import numpy as np
import ml_dtypes


BF16 = ml_dtypes.bfloat16


def bf(x):
    return np.asarray(x, np.float32).astype(BF16)


def f64(x):
    return np.asarray(x).astype(np.float64)


E2M1 = np.array([0.0, 0.5, 1.0, 1.5, 2.0, 3.0, 4.0, 6.0, -0.0, -0.5, -1.0, -1.5, -2.0, -3.0, -4.0, -6.0])


def pack_weight(w, fmt):
    k, n = w.shape
    w = f64(bf(w)).reshape(k // 32, 32, n)
    amax = np.abs(w).max(1)
    if fmt == "e4m3":
        byte = np.frexp(amax)[1] - 1 + 127 - 7
    else:
        mant, ex = np.frexp(amax / 6.0)
        byte = np.where(mant > 0.5, ex, ex - 1) + 127
    byte = np.clip(np.where(amax > 0, byte, 1), 1, 254)
    scaled = (w * np.exp2(127.0 - byte)[:, None, :]).reshape(k, n).astype(np.float32)
    by_word = np.ascontiguousarray(scaled.reshape(k // 512, 128, 4, n).transpose(0, 1, 3, 2))
    if fmt == "e4m3":
        words = by_word.astype(ml_dtypes.float8_e4m3fn).view(np.uint8)
    else:
        c = by_word.astype(ml_dtypes.float4_e2m1fn).view(np.uint8) & 0xF
        words = c[..., 0::2] | (c[..., 1::2] << 4)
    return np.ascontiguousarray(words), np.ascontiguousarray(byte.astype(np.uint8).reshape(k // 512, 16, n))


def unpack_weight(words, scales, fmt):
    g, p, n, _ = words.shape
    if fmt == "e4m3":
        vals = np.ascontiguousarray(words).view(ml_dtypes.float8_e4m3fn).astype(np.float64)
    else:
        nib = np.empty((g, p, n, 4), np.uint8)
        nib[..., 0::2] = words & 0xF
        nib[..., 1::2] = words >> 4
        vals = E2M1[nib]
    vals = vals * np.repeat(np.exp2(scales.astype(np.float64) - 127.0), 8, axis=1)[..., None]
    return vals.transpose(0, 1, 3, 2).reshape(g * 512, n)

def pack4(w):
    words, scales = pack_weight(w, "e2m1")
    return words.reshape(words.shape[0], 128, -1), scales


def unpack4(words, scales):
    return unpack_weight(words.reshape(words.shape[0], 128, -1, 2), scales, "e2m1")


def kspread(k):
    return np.exp2(np.repeat(np.random.randint(-6, 7, k // 32), 32).astype(np.float64))


B, S, H, D = 2, 256, 16, 256
E = H * D
HALF = D // 2


def rotate_half(u):
    u1, u2 = np.split(u, 2, axis=-1)
    return np.concatenate([-u2, u1], axis=-1)


def apply_rope(t, sin, cos):
    x1, x2 = np.split(t, 2, axis=-1)
    x_rot = x1 * cos + rotate_half(x1) * sin
    return np.concatenate([x_rot, x2], axis=-1)


def setup_inputs():
    s = kspread(E)
    th = np.random.uniform(0.0, 2.0 * np.pi, (S, HALF))
    x = np.random.standard_normal((B, S, E)) * s
    x_words, x_scales = pack4(x.reshape(B * S, E).T)
    words, scales = pack4(np.random.standard_normal((E, 3 * E)) / np.sqrt(E) / s[:, None])
    return {"x_words": x_words,
            "x_scales": x_scales,
            "W_qkv_words": words,
            "W_qkv_scales": scales,
            "b_qkv": bf(np.random.standard_normal(3 * E) * 0.2),
            "sin_tab": bf(np.sin(th)),
            "cos_tab": bf(np.cos(th))}


def reference(x_words, x_scales, W_qkv_words, W_qkv_scales, b_qkv, sin_tab, cos_tab):
    qkv = (unpack4(x_words, x_scales).T.reshape(B, S, E) @ unpack4(W_qkv_words, W_qkv_scales)) + f64(b_qkv)
    q, k, v = np.split(qkv, 3, axis=-1)
    q = q.reshape(B, S, H, D)
    k = k.reshape(B, S, H, D)
    v = v.reshape(B, S, H, D)
    sin = f64(sin_tab)[None, :, None, :]
    cos = f64(cos_tab)[None, :, None, :]
    q_rot = apply_rope(q, sin, cos)
    k_rot = apply_rope(k, sin, cos)
    return q_rot, k_rot, v

@@ -1,0 +1,203 @@
+from contextlib import ExitStack
+
+import concourse.mybir as mybir
+
+FLOPS = 2 * 512 * 4096 * 12288
+
+F32 = mybir.dt.float32
+BF16 = mybir.dt.bfloat16
+U8 = mybir.dt.uint8
+I32 = mybir.dt.int32
+FP4X4 = mybir.dt.float4_e2m1fn_x4
+ADD = mybir.AluOpType.add
+MULT = mybir.AluOpType.mult
+
+P = 128
+PASSES = 8
+TOKEN_TILES = 4
+BANK = 512
+CHUNK = 1024
+BANKS_PER_CHUNK = CHUNK // BANK
+THIRD = 4096
+CHUNKS_PER_THIRD = THIRD // CHUNK
+W_BUFS = 5
+HEAD_RUNS = ((0, 1), (1, 4), (4, 8))
+QUADRANT_ORDER = (0, 2, 1, 3)
+
+
+def tile_improvedattention_pa_kernel(
+    tc, x_words, x_scales, W_qkv_words, W_qkv_scales, b_qkv, sin_tab, cos_tab, out_0, out_1, out_2
+):
+    nc = tc.nc
+    outs = [o.rearrange("b s h d -> (b s) (h d)") for o in (out_0, out_1, out_2)]
+    chunks = [(third, CHUNK * i) for i in range(CHUNKS_PER_THIRD) for third in range(3)]
+
+    with ExitStack() as ctx:
+        keep = ctx.enter_context(tc.tile_pool(name="keep", bufs=1))
+        opool = ctx.enter_context(tc.tile_pool(name="opool", bufs=6))
+        tpool = ctx.enter_context(tc.tile_pool(name="tpool", bufs=3))
+        psum = ctx.enter_context(tc.psum_pool(name="psum", bufs=8))
+        ctx.enter_context(tc.manual_schedule())
+
+        def load_codes(dst, words, g0, g1, b0, b1):
+            nc.sync.dma_start(
+                out=dst.bitcast(I32),
+                in_=words[g0:g1, :, b0:b1].rearrange("g p n -> p g n").bitcast(I32),
+            )
+
+        def load_scales(dst, scales, g0, g1, c0, c1):
+            for q in QUADRANT_ORDER:
+                nc.sync.dma_start(
+                    out=dst[32 * q : 32 * q + 4, :, :].bitcast(I32),
+                    in_=scales[g0:g1, 4 * q : 4 * q + 4, c0:c1].rearrange("g r n -> r g n").bitcast(I32),
+                )
+
+        def zero(plane):
+            nc.vector.memset(plane[:].bitcast(I32), 0)
+
+        def w_col(j):
+            third, c0 = chunks[j]
+            return THIRD * third + c0
+
+        x_codes = []
+        w0_codes = []
+        w0_planes = []
+        for r, (g0, g1) in enumerate(HEAD_RUNS):
+            xc = keep.tile([P, g1 - g0, 2 * 512], U8, name="xc%d" % r, align_bytes=256)
+            x_codes.append(xc)
+            wc0 = keep.tile([P, g1 - g0, 2 * CHUNK], U8, name="w0c%d" % r, align_bytes=256)
+            w0_codes.append(wc0)
+            ws0 = keep.tile([P, g1 - g0, CHUNK], U8, name="w0s%d" % r, align_bytes=256)
+            w0_planes.append(ws0)
+        x_planes = keep.tile([P, PASSES, 512], U8, name="xs", align_bytes=256)
+        w_codes = []
+        w_planes = []
+        for b in range(W_BUFS):
+            wcb = keep.tile([P, PASSES, 2 * CHUNK], U8, name="wc%d" % b, align_bytes=256)
+            w_codes.append(wcb)
+            wsb = keep.tile([P, PASSES, CHUNK], U8, name="ws%d" % b, align_bytes=256)
+            w_planes.append(wsb)
+        bias = []
+        for j in range(len(chunks)):
+            bj = keep.tile([P, CHUNK], BF16, name="bias%d" % j)
+            bias.append(bj)
+        cos_bf = keep.tile([P, 2, 128], BF16, name="cos_bf")
+        sin_bf = keep.tile([P, 2, 128], BF16, name="sin_bf")
+        cos2 = keep.tile([P, 2, 2, 128], F32, name="cos2")
+        sin2 = keep.tile([P, 2, 2, 128], F32, name="sin2")
+
+        def run_of(g):
+            for r, (g0, g1) in enumerate(HEAD_RUNS):
+                if g0 <= g < g1:
+                    return r, g - g0
+            raise ValueError("no such pass")
+
+        def load_bias(j):
+            c0 = w_col(j)
+            nc.sync.dma_start(out=bias[j][:], in_=b_qkv[c0 : c0 + CHUNK].partition_broadcast(P))
+
+        def load_chunk(j):
+            b = (j - 1) % W_BUFS
+            c0 = w_col(j)
+            load_scales(w_planes[b], W_qkv_scales, 0, PASSES, c0, c0 + CHUNK)
+            load_codes(w_codes[b][:], W_qkv_words, 0, PASSES, 2 * c0, 2 * (c0 + CHUNK))
+            load_bias(j)
+
+        zero(w0_planes[0])
+        zero(x_planes)
+        zero(w0_planes[1])
+        zero(w0_planes[2])
+        for b in range(W_BUFS):
+            zero(w_planes[b])
+
+        nc.gpsimd.dma_start(out=cos_bf[:], in_=cos_tab.rearrange("(t p) j -> p t j", p=P))
+        nc.gpsimd.dma_start(out=sin_bf[:], in_=sin_tab.rearrange("(t p) j -> p t j", p=P))
+        for h in range(2):
+            nc.gpsimd.tensor_copy(out=cos2[:, :, h, :], in_=cos_bf[:])
+            nc.gpsimd.tensor_scalar(
+                out=sin2[:, :, h, 0:64], in0=sin_bf[:, :, 0:64], scalar1=-1.0, scalar2=0.0, op0=MULT, op1=ADD
+            )
+            nc.gpsimd.tensor_copy(out=sin2[:, :, h, 64:128], in_=sin_bf[:, :, 64:128])
+
+        c00 = w_col(0)
+        for r, (g0, g1) in enumerate(HEAD_RUNS):
+            if r == 0:
+                load_codes(x_codes[r][:], x_words, g0, g1, 0, 1024)
+                load_codes(w0_codes[r][:], W_qkv_words, g0, g1, 2 * c00, 2 * (c00 + CHUNK))
+                load_scales(w0_planes[r], W_qkv_scales, g0, g1, c00, c00 + CHUNK)
+                load_scales(x_planes, x_scales, 0, PASSES, 0, 512)
+            else:
+                load_scales(w0_planes[r], W_qkv_scales, g0, g1, c00, c00 + CHUNK)
+                load_codes(x_codes[r][:], x_words, g0, g1, 0, 1024)
+                load_codes(w0_codes[r][:], W_qkv_words, g0, g1, 2 * c00, 2 * (c00 + CHUNK))
+        load_bias(0)
+        for j in range(1, 1 + W_BUFS):
+            load_chunk(j)
+
+        def one_pass(acc, j, g, m, nb):
+            r, gi = run_of(g)
+            if j == 0:
+                codes = w0_codes[r][:, gi, 2 * BANK * nb : 2 * BANK * (nb + 1)]
+                plane = w0_planes[r][:, gi, BANK * nb : BANK * (nb + 1)]
+            else:
+                b = (j - 1) % W_BUFS
+                codes = w_codes[b][:, g, 2 * BANK * nb : 2 * BANK * (nb + 1)]
+                plane = w_planes[b][:, g, BANK * nb : BANK * (nb + 1)]
+            nc.tensor.matmul_mx(
+                out=acc[:],
+                lhsT=x_codes[r][:, gi, 2 * P * m : 2 * P * (m + 1)].bitcast(FP4X4),
+                lhsT_scale=x_planes[:, g, P * m : P * (m + 1)],
+                rhs=codes.bitcast(FP4X4),
+                rhs_scale=plane,
+                start=(g == 0),
+                stop=(g == PASSES - 1),
+            )
+
+        pending = []
+
+        def finish_pending():
+            for o, t, third, m, c0 in pending:
+                if t is not None:
+                    ov = o[:].rearrange("p (h d) -> p h d", d=256)
+                    nc.vector.tensor_tensor(out=ov[:, :, 0:128], in0=ov[:, :, 0:128], in1=t[:], op=ADD)
+                nc.scalar.dma_start(out=outs[third][P * m : P * (m + 1), c0 : c0 + BANK], in_=o[:])
+            pending.clear()
+
+        def way_out(acc, j, m, nb):
+            third, c0 = chunks[j]
+            o = opool.tile([P, BANK], F32, name="o")
+            nc.vector.tensor_tensor(out=o[:], in0=acc[:], in1=bias[j][:, BANK * nb : BANK * (nb + 1)], op=ADD)
+            finish_pending()
+            t = None
+            if third < 2:
+                pt = m % 2
+                ov = o[:].rearrange("p (h d) -> p h d", d=256)
+                t = tpool.tile([P, 2, 128], F32, name="t")
+                nc.vector.tensor_tensor(out=t[:, :, 0:64], in0=ov[:, :, 64:128], in1=sin2[:, pt, :, 0:64], op=MULT)
+                nc.vector.tensor_tensor(out=t[:, :, 64:128], in0=ov[:, :, 0:64], in1=sin2[:, pt, :, 64:128], op=MULT)
+                nc.vector.tensor_tensor(out=ov[:, :, 0:128], in0=ov[:, :, 0:128], in1=cos2[:, pt, :, :], op=MULT)
+            pending.append((o, t, third, m, c0 + BANK * nb))
+
+        accs = []
+        for m in range(TOKEN_TILES):
+            for nb in range(BANKS_PER_CHUNK):
+                acc = psum.tile([P, BANK], F32, name="acc")
+                accs.append(acc)
+        for g in range(PASSES):
+            for m in range(TOKEN_TILES):
+                for nb in range(BANKS_PER_CHUNK):
+                    one_pass(accs[BANKS_PER_CHUNK * m + nb], 0, g, m, nb)
+        for m in range(TOKEN_TILES):
+            for nb in range(BANKS_PER_CHUNK):
+                way_out(accs[BANKS_PER_CHUNK * m + nb], 0, m, nb)
+
+        for j in range(1, len(chunks)):
+            for m in range(TOKEN_TILES):
+                for nb in range(BANKS_PER_CHUNK):
+                    acc = psum.tile([P, BANK], F32, name="acc")
+                    for g in range(PASSES):
+                        one_pass(acc, j, g, m, nb)
+                    way_out(acc, j, m, nb)
+            if j + W_BUFS < len(chunks):
+                load_chunk(j + W_BUFS)
+        finish_pending()

@@ -23,6 +23,7 @@ CHUNKS_PER_THIRD = THIRD // CHUNK
 W_BUFS = 5
 HEAD_RUNS = ((0, 1), (1, 4), (4, 8))
 QUADRANT_ORDER = (0, 2, 1, 3)
+WARM_UP = 8
 
 
 def tile_improvedattention_pa_kernel(
@@ -85,6 +86,7 @@ def tile_improvedattention_pa_kernel(
         sin_bf = keep.tile([P, 2, 128], BF16, name="sin_bf")
         cos2 = keep.tile([P, 2, 2, 128], F32, name="cos2")
         sin2 = keep.tile([P, 2, 2, 128], F32, name="sin2")
+        warm = keep.tile([P, BANK], BF16, name="warm")
 
         def run_of(g):
             for r, (g0, g1) in enumerate(HEAD_RUNS):
@@ -103,12 +105,17 @@ def tile_improvedattention_pa_kernel(
             load_codes(w_codes[b][:], W_qkv_words, 0, PASSES, 2 * c0, 2 * (c0 + CHUNK))
             load_bias(j)
 
-        zero(w0_planes[0])
+        nc.gpsimd.memset(w0_planes[0][:].bitcast(F32), 0.0)
+        zero(warm)
         zero(x_planes)
         zero(w0_planes[1])
         zero(w0_planes[2])
         for b in range(W_BUFS):
             zero(w_planes[b])
+
+        idle = psum.tile([P, BANK], F32, name="acc")
+        for i in range(WARM_UP):
+            nc.tensor.matmul(out=idle[:], lhsT=warm[:, 0:P], rhs=warm[:], start=True, stop=True)
 
         nc.gpsimd.dma_start(out=cos_bf[:], in_=cos_tab.rearrange("(t p) j -> p t j", p=P))
         nc.gpsimd.dma_start(out=sin_bf[:], in_=sin_tab.rearrange("(t p) j -> p t j", p=P))
@@ -134,17 +141,17 @@ def tile_improvedattention_pa_kernel(
         for j in range(1, 1 + W_BUFS):
             load_chunk(j)
 
-        def one_pass(acc, j, g, m, nb):
+        def one_pass(acc, j, g, m, c0, width):
             r, gi = run_of(g)
             if j == 0:
-                codes = w0_codes[r][:, gi, 2 * BANK * nb : 2 * BANK * (nb + 1)]
-                plane = w0_planes[r][:, gi, BANK * nb : BANK * (nb + 1)]
+                codes = w0_codes[r][:, gi, 2 * c0 : 2 * (c0 + width)]
+                plane = w0_planes[r][:, gi, c0 : c0 + width]
             else:
                 b = (j - 1) % W_BUFS
-                codes = w_codes[b][:, g, 2 * BANK * nb : 2 * BANK * (nb + 1)]
-                plane = w_planes[b][:, g, BANK * nb : BANK * (nb + 1)]
+                codes = w_codes[b][:, g, 2 * c0 : 2 * (c0 + width)]
+                plane = w_planes[b][:, g, c0 : c0 + width]
             nc.tensor.matmul_mx(
-                out=acc[:],
+                out=acc[:, 0:width],
                 lhsT=x_codes[r][:, gi, 2 * P * m : 2 * P * (m + 1)].bitcast(FP4X4),
                 lhsT_scale=x_planes[:, g, P * m : P * (m + 1)],
                 rhs=codes.bitcast(FP4X4),
@@ -156,17 +163,17 @@ def tile_improvedattention_pa_kernel(
         pending = []
 
         def finish_pending():
-            for o, t, third, m, c0 in pending:
+            for o, t, third, m, c0, width in pending:
                 if t is not None:
                     ov = o[:].rearrange("p (h d) -> p h d", d=256)
                     nc.vector.tensor_tensor(out=ov[:, :, 0:128], in0=ov[:, :, 0:128], in1=t[:], op=ADD)
-                nc.scalar.dma_start(out=outs[third][P * m : P * (m + 1), c0 : c0 + BANK], in_=o[:])
+                nc.scalar.dma_start(out=outs[third][P * m : P * (m + 1), c0 : c0 + width], in_=o[:, 0:width])
             pending.clear()
 
-        def way_out(acc, j, m, nb):
-            third, c0 = chunks[j]
+        def way_out(acc, j, m, c0, width):
+            third, first = chunks[j]
             o = opool.tile([P, BANK], F32, name="o")
-            nc.vector.tensor_tensor(out=o[:], in0=acc[:], in1=bias[j][:, BANK * nb : BANK * (nb + 1)], op=ADD)
+            nc.vector.tensor_tensor(out=o[:, 0:width], in0=acc[:, 0:width], in1=bias[j][:, c0 : c0 + width], op=ADD)
             finish_pending()
             t = None
             if third < 2:
@@ -176,7 +183,7 @@ def tile_improvedattention_pa_kernel(
                 nc.vector.tensor_tensor(out=t[:, :, 0:64], in0=ov[:, :, 64:128], in1=sin2[:, pt, :, 0:64], op=MULT)
                 nc.vector.tensor_tensor(out=t[:, :, 64:128], in0=ov[:, :, 0:64], in1=sin2[:, pt, :, 64:128], op=MULT)
                 nc.vector.tensor_tensor(out=ov[:, :, 0:128], in0=ov[:, :, 0:128], in1=cos2[:, pt, :, :], op=MULT)
-            pending.append((o, t, third, m, c0 + BANK * nb))
+            pending.append((o, t, third, m, first + c0, width))
 
         accs = []
         for m in range(TOKEN_TILES):
@@ -186,18 +193,22 @@ def tile_improvedattention_pa_kernel(
         for g in range(PASSES):
             for m in range(TOKEN_TILES):
                 for nb in range(BANKS_PER_CHUNK):
-                    one_pass(accs[BANKS_PER_CHUNK * m + nb], 0, g, m, nb)
+                    one_pass(accs[BANKS_PER_CHUNK * m + nb], 0, g, m, BANK * nb, BANK)
         for m in range(TOKEN_TILES):
             for nb in range(BANKS_PER_CHUNK):
-                way_out(accs[BANKS_PER_CHUNK * m + nb], 0, m, nb)
+                way_out(accs[BANKS_PER_CHUNK * m + nb], 0, m, BANK * nb, BANK)
 
+        last = len(chunks) - 1
         for j in range(1, len(chunks)):
             for m in range(TOKEN_TILES):
                 for nb in range(BANKS_PER_CHUNK):
-                    acc = psum.tile([P, BANK], F32, name="acc")
-                    for g in range(PASSES):
-                        one_pass(acc, j, g, m, nb)
-                    way_out(acc, j, m, nb)
+                    at_end = j == last and m == TOKEN_TILES - 1 and nb == BANKS_PER_CHUNK - 1
+                    width = BANK // 2 if at_end else BANK
+                    for c0 in range(BANK * nb, BANK * (nb + 1), width):
+                        acc = psum.tile([P, BANK], F32, name="acc")
+                        for g in range(PASSES):
+                            one_pass(acc, j, g, m, c0, width)
+                        way_out(acc, j, m, c0, width)
             if j + W_BUFS < len(chunks):
                 load_chunk(j + W_BUFS)
         finish_pending()

@@ -24,6 +24,7 @@ W_BUFS = 5
 HEAD_RUNS = ((0, 1), (1, 4), (4, 8))
 QUADRANT_ORDER = (0, 2, 1, 3)
 WARM_UP = 8
+GROUP = 4
 
 
 def tile_improvedattention_pa_kernel(
@@ -35,9 +36,9 @@ def tile_improvedattention_pa_kernel(
 
     with ExitStack() as ctx:
         keep = ctx.enter_context(tc.tile_pool(name="keep", bufs=1))
-        opool = ctx.enter_context(tc.tile_pool(name="opool", bufs=6))
-        tpool = ctx.enter_context(tc.tile_pool(name="tpool", bufs=3))
-        psum = ctx.enter_context(tc.psum_pool(name="psum", bufs=8))
+        opool = ctx.enter_context(tc.tile_pool(name="opool", bufs=3))
+        tpool = ctx.enter_context(tc.tile_pool(name="tpool", bufs=2))
+        psum = ctx.enter_context(tc.psum_pool(name="psum", bufs=2))
         ctx.enter_context(tc.manual_schedule())
 
         def load_codes(dst, words, g0, g1, b0, b1):
@@ -84,8 +85,8 @@ def tile_improvedattention_pa_kernel(
             bias.append(bj)
         cos_bf = keep.tile([P, 2, 128], BF16, name="cos_bf")
         sin_bf = keep.tile([P, 2, 128], BF16, name="sin_bf")
-        cos2 = keep.tile([P, 2, 2, 128], F32, name="cos2")
-        sin2 = keep.tile([P, 2, 2, 128], F32, name="sin2")
+        cos_rep = keep.tile([P, 2, 4, 128], F32, name="cos_rep")
+        sin_rep = keep.tile([P, 2, 4, 128], F32, name="sin_rep")
         warm = keep.tile([P, BANK], BF16, name="warm")
 
         def run_of(g):
@@ -119,12 +120,14 @@ def tile_improvedattention_pa_kernel(
 
         nc.gpsimd.dma_start(out=cos_bf[:], in_=cos_tab.rearrange("(t p) j -> p t j", p=P))
         nc.gpsimd.dma_start(out=sin_bf[:], in_=sin_tab.rearrange("(t p) j -> p t j", p=P))
-        for h in range(2):
-            nc.gpsimd.tensor_copy(out=cos2[:, :, h, :], in_=cos_bf[:])
+        for h in range(4):
+            nc.gpsimd.tensor_copy(out=cos_rep[:, :, h, :], in_=cos_bf[:])
             nc.gpsimd.tensor_scalar(
-                out=sin2[:, :, h, 0:64], in0=sin_bf[:, :, 0:64], scalar1=-1.0, scalar2=0.0, op0=MULT, op1=ADD
+                out=sin_rep[:, :, h, 0:64], in0=sin_bf[:, :, 0:64], scalar1=-1.0, scalar2=0.0, op0=MULT, op1=ADD
             )
-            nc.gpsimd.tensor_copy(out=sin2[:, :, h, 64:128], in_=sin_bf[:, :, 64:128])
+            nc.gpsimd.tensor_copy(out=sin_rep[:, :, h, 64:128], in_=sin_bf[:, :, 64:128])
+        cos8 = cos_rep[:].rearrange("p t k j -> p (t k) j")
+        sin8 = sin_rep[:].rearrange("p t k j -> p (t k) j")
 
         c00 = w_col(0)
         for r, (g0, g1) in enumerate(HEAD_RUNS):
@@ -151,7 +154,7 @@ def tile_improvedattention_pa_kernel(
                 codes = w_codes[b][:, g, 2 * c0 : 2 * (c0 + width)]
                 plane = w_planes[b][:, g, c0 : c0 + width]
             nc.tensor.matmul_mx(
-                out=acc[:, 0:width],
+                out=acc,
                 lhsT=x_codes[r][:, gi, 2 * P * m : 2 * P * (m + 1)].bitcast(FP4X4),
                 lhsT_scale=x_planes[:, g, P * m : P * (m + 1)],
                 rhs=codes.bitcast(FP4X4),
@@ -160,55 +163,74 @@ def tile_improvedattention_pa_kernel(
                 stop=(g == PASSES - 1),
             )
 
-        pending = []
+        def group_passes(grp, j, a, g0, g1, pass_outer):
+            if pass_outer:
+                order = [(g, i) for g in range(g0, g1) for i in range(GROUP)]
+            else:
+                order = [(g, i) for i in range(GROUP) for g in range(g0, g1)]
+            for g, i in order:
+                one_pass(grp[:, i, :], j, g, 2 * a + i // 2, BANK * (i % 2), BANK)
 
-        def finish_pending():
-            for o, t, third, m, c0, width in pending:
-                if t is not None:
-                    ov = o[:].rearrange("p (h d) -> p h d", d=256)
-                    nc.vector.tensor_tensor(out=ov[:, :, 0:128], in0=ov[:, :, 0:128], in1=t[:], op=ADD)
-                nc.scalar.dma_start(out=outs[third][P * m : P * (m + 1), c0 : c0 + width], in_=o[:, 0:width])
-            pending.clear()
-
-        def way_out(acc, j, m, c0, width):
+        def group_out(grp, j, a):
             third, first = chunks[j]
-            o = opool.tile([P, BANK], F32, name="o")
-            nc.vector.tensor_tensor(out=o[:, 0:width], in0=acc[:, 0:width], in1=bias[j][:, c0 : c0 + width], op=ADD)
-            finish_pending()
-            t = None
+            o = opool.tile([P, GROUP, BANK], F32, name="o")
+            for i in range(GROUP):
+                nc.vector.tensor_tensor(
+                    out=o[:, i, :], in0=grp[:, i, :], in1=bias[j][:, BANK * (i % 2) : BANK * (i % 2 + 1)], op=ADD
+                )
             if third < 2:
-                pt = m % 2
-                ov = o[:].rearrange("p (h d) -> p h d", d=256)
-                t = tpool.tile([P, 2, 128], F32, name="t")
-                nc.vector.tensor_tensor(out=t[:, :, 0:64], in0=ov[:, :, 64:128], in1=sin2[:, pt, :, 0:64], op=MULT)
-                nc.vector.tensor_tensor(out=t[:, :, 64:128], in0=ov[:, :, 0:64], in1=sin2[:, pt, :, 64:128], op=MULT)
-                nc.vector.tensor_tensor(out=ov[:, :, 0:128], in0=ov[:, :, 0:128], in1=cos2[:, pt, :, :], op=MULT)
-            pending.append((o, t, third, m, first + c0, width))
+                ov = o[:].rearrange("p i (h d) -> p (i h) d", d=256)
+                t = tpool.tile([P, 2 * GROUP, 128], F32, name="t")
+                nc.vector.tensor_tensor(out=t[:, :, 0:64], in0=ov[:, :, 64:128], in1=sin8[:, :, 0:64], op=MULT)
+                nc.vector.tensor_tensor(out=t[:, :, 64:128], in0=ov[:, :, 0:64], in1=sin8[:, :, 64:128], op=MULT)
+                nc.vector.tensor_tensor(out=ov[:, :, 0:128], in0=ov[:, :, 0:128], in1=cos8, op=MULT)
+                nc.vector.tensor_tensor(out=ov[:, :, 0:128], in0=ov[:, :, 0:128], in1=t[:], op=ADD)
+            for mi in range(2):
+                m = 2 * a + mi
+                nc.scalar.dma_start(
+                    out=outs[third][P * m : P * (m + 1), first : first + CHUNK],
+                    in_=o[:, 2 * mi : 2 * mi + 2, :].rearrange("p i c -> p (i c)"),
+                )
 
-        accs = []
-        for m in range(TOKEN_TILES):
-            for nb in range(BANKS_PER_CHUNK):
-                acc = psum.tile([P, BANK], F32, name="acc")
-                accs.append(acc)
-        for g in range(PASSES):
-            for m in range(TOKEN_TILES):
-                for nb in range(BANKS_PER_CHUNK):
-                    one_pass(accs[BANKS_PER_CHUNK * m + nb], 0, g, m, BANK * nb, BANK)
-        for m in range(TOKEN_TILES):
-            for nb in range(BANKS_PER_CHUNK):
-                way_out(accs[BANKS_PER_CHUNK * m + nb], 0, m, BANK * nb, BANK)
+        grp_a = psum.tile([P, GROUP, BANK], F32, name="acc")
+        grp_b = psum.tile([P, GROUP, BANK], F32, name="acc")
+        half = PASSES // 2
+        for g in range(half):
+            group_passes(grp_a, 0, 0, g, g + 1, True)
+            group_passes(grp_b, 0, 1, g, g + 1, True)
+        group_passes(grp_a, 0, 0, half, PASSES, True)
+        group_out(grp_a, 0, 0)
+        group_passes(grp_b, 0, 1, half, PASSES, True)
+        group_out(grp_b, 0, 1)
 
         last = len(chunks) - 1
         for j in range(1, len(chunks)):
-            for m in range(TOKEN_TILES):
-                for nb in range(BANKS_PER_CHUNK):
-                    at_end = j == last and m == TOKEN_TILES - 1 and nb == BANKS_PER_CHUNK - 1
-                    width = BANK // 2 if at_end else BANK
-                    for c0 in range(BANK * nb, BANK * (nb + 1), width):
-                        acc = psum.tile([P, BANK], F32, name="acc")
-                        for g in range(PASSES):
-                            one_pass(acc, j, g, m, c0, width)
-                        way_out(acc, j, m, c0, width)
+            for a in range(TOKEN_TILES // 2):
+                if j == last and a == TOKEN_TILES // 2 - 1:
+                    continue
+                grp = psum.tile([P, GROUP, BANK], F32, name="acc")
+                group_passes(grp, j, a, 0, PASSES, False)
+                group_out(grp, j, a)
             if j + W_BUFS < len(chunks):
                 load_chunk(j + W_BUFS)
-        finish_pending()
+
+        third, first = chunks[last]
+        tail = [
+            [(2, 0, BANK), (2, BANK, BANK)],
+            [(3, 0, BANK)],
+            [(3, BANK, BANK // 2)],
+            [(3, BANK + BANK // 2, BANK // 2)],
+        ]
+        for pieces in tail:
+            acc = psum.tile([P, len(pieces), BANK], F32, name="acc")
+            for i, (m, c0, width) in enumerate(pieces):
+                for g in range(PASSES):
+                    one_pass(acc[:, i, 0:width], last, g, m, c0, width)
+            o = opool.tile([P, len(pieces), BANK], F32, name="o")
+            for i, (m, c0, width) in enumerate(pieces):
+                nc.vector.tensor_tensor(
+                    out=o[:, i, 0:width], in0=acc[:, i, 0:width], in1=bias[last][:, c0 : c0 + width], op=ADD
+                )
+                nc.scalar.dma_start(
+                    out=outs[third][P * m : P * (m + 1), first + c0 : first + c0 + width], in_=o[:, i, 0:width]
+                )

@@ -21,7 +21,8 @@ BANKS_PER_CHUNK = CHUNK // BANK
 THIRD = 4096
 CHUNKS_PER_THIRD = THIRD // CHUNK
 W_BUFS = 5
-HEAD_RUNS = ((0, 1), (1, 4), (4, 8))
+CODE_RUNS = ((0, 1), (1, 2), (2, 4), (4, 8))
+PLANE_RUNS = ((0, 1), (1, 4), (4, 8))
 QUADRANT_ORDER = (0, 2, 1, 3)
 WARM_UP = 8
 GROUP = 4
@@ -47,8 +48,8 @@ def tile_improvedattention_pa_kernel(
                 in_=words[g0:g1, :, b0:b1].rearrange("g p n -> p g n").bitcast(I32),
             )
 
-        def load_scales(dst, scales, g0, g1, c0, c1):
-            for q in QUADRANT_ORDER:
+        def load_scales(dst, scales, g0, g1, c0, c1, quadrants=QUADRANT_ORDER):
+            for q in quadrants:
                 nc.sync.dma_start(
                     out=dst[32 * q : 32 * q + 4, :, :].bitcast(I32),
                     in_=scales[g0:g1, 4 * q : 4 * q + 4, c0:c1].rearrange("g r n -> r g n").bitcast(I32),
@@ -64,11 +65,12 @@ def tile_improvedattention_pa_kernel(
         x_codes = []
         w0_codes = []
         w0_planes = []
-        for r, (g0, g1) in enumerate(HEAD_RUNS):
+        for r, (g0, g1) in enumerate(CODE_RUNS):
             xc = keep.tile([P, g1 - g0, 2 * 512], U8, name="xc%d" % r, align_bytes=256)
             x_codes.append(xc)
             wc0 = keep.tile([P, g1 - g0, 2 * CHUNK], U8, name="w0c%d" % r, align_bytes=256)
             w0_codes.append(wc0)
+        for r, (g0, g1) in enumerate(PLANE_RUNS):
             ws0 = keep.tile([P, g1 - g0, CHUNK], U8, name="w0s%d" % r, align_bytes=256)
             w0_planes.append(ws0)
         x_planes = keep.tile([P, PASSES, 512], U8, name="xs", align_bytes=256)
@@ -89,8 +91,8 @@ def tile_improvedattention_pa_kernel(
         sin_rep = keep.tile([P, 2, 4, 128], F32, name="sin_rep")
         warm = keep.tile([P, BANK], BF16, name="warm")
 
-        def run_of(g):
-            for r, (g0, g1) in enumerate(HEAD_RUNS):
+        def run_of(runs, g):
+            for r, (g0, g1) in enumerate(runs):
                 if g0 <= g < g1:
                     return r, g - g0
             raise ValueError("no such pass")
@@ -106,7 +108,6 @@ def tile_improvedattention_pa_kernel(
             load_codes(w_codes[b][:], W_qkv_words, 0, PASSES, 2 * c0, 2 * (c0 + CHUNK))
             load_bias(j)
 
-        nc.gpsimd.memset(w0_planes[0][:].bitcast(F32), 0.0)
         zero(warm)
         zero(x_planes)
         zero(w0_planes[1])
@@ -130,25 +131,42 @@ def tile_improvedattention_pa_kernel(
         sin8 = sin_rep[:].rearrange("p t k j -> p (t k) j")
 
         c00 = w_col(0)
-        for r, (g0, g1) in enumerate(HEAD_RUNS):
-            if r == 0:
-                load_codes(x_codes[r][:], x_words, g0, g1, 0, 1024)
-                load_codes(w0_codes[r][:], W_qkv_words, g0, g1, 2 * c00, 2 * (c00 + CHUNK))
-                load_scales(w0_planes[r], W_qkv_scales, g0, g1, c00, c00 + CHUNK)
-                load_scales(x_planes, x_scales, 0, PASSES, 0, 512)
-            else:
-                load_scales(w0_planes[r], W_qkv_scales, g0, g1, c00, c00 + CHUNK)
-                load_codes(x_codes[r][:], x_words, g0, g1, 0, 1024)
-                load_codes(w0_codes[r][:], W_qkv_words, g0, g1, 2 * c00, 2 * (c00 + CHUNK))
+        def head_codes(r):
+            g0, g1 = CODE_RUNS[r]
+            load_codes(x_codes[r][:], x_words, g0, g1, 0, 1024)
+            load_codes(w0_codes[r][:], W_qkv_words, g0, g1, 2 * c00, 2 * (c00 + CHUNK))
+
+        def head_planes(r, quadrants=QUADRANT_ORDER):
+            g0, g1 = PLANE_RUNS[r]
+            load_scales(w0_planes[r], W_qkv_scales, g0, g1, c00, c00 + CHUNK, quadrants)
+
+        def first_plane(quadrants):
+            rows = W_qkv_scales.rearrange("g r n -> (g r) n")
+            for q in quadrants:
+                nc.sync.dma_start(
+                    out=w0_planes[0][32 * q : 32 * q + 32, 0, :].bitcast(I32),
+                    in_=rows[4 * q : 4 * q + 32, c00 : c00 + CHUNK].bitcast(I32),
+                )
+
+        first_plane(QUADRANT_ORDER[0:2])
+        head_codes(0)
+        first_plane(QUADRANT_ORDER[2:4])
+        load_scales(x_planes, x_scales, 0, PASSES, 0, 512)
+        head_codes(1)
+        head_planes(1)
+        head_codes(2)
+        head_planes(2)
+        head_codes(3)
         load_bias(0)
         for j in range(1, 1 + W_BUFS):
             load_chunk(j)
 
         def one_pass(acc, j, g, m, c0, width):
-            r, gi = run_of(g)
+            r, gi = run_of(CODE_RUNS, g)
             if j == 0:
+                rp, gp = run_of(PLANE_RUNS, g)
                 codes = w0_codes[r][:, gi, 2 * c0 : 2 * (c0 + width)]
-                plane = w0_planes[r][:, gi, c0 : c0 + width]
+                plane = w0_planes[rp][:, gp, c0 : c0 + width]
             else:
                 b = (j - 1) % W_BUFS
                 codes = w_codes[b][:, g, 2 * c0 : 2 * (c0 + width)]

@@ -106,7 +106,7 @@ def tile_improvedattention_pa_kernel(
             c0 = w_col(j)
             load_scales(w_planes[b], W_qkv_scales, 0, PASSES, c0, c0 + CHUNK)
             load_codes(w_codes[b][:], W_qkv_words, 0, PASSES, 2 * c0, 2 * (c0 + CHUNK))
-            load_bias(j)
+            load_bias(j - 1)
 
         zero(warm)
         zero(x_planes)
@@ -115,6 +115,8 @@ def tile_improvedattention_pa_kernel(
         for b in range(W_BUFS):
             zero(w_planes[b])
 
+        first_copy = keep.tile([P, 2], BF16, name="first_copy")
+        nc.scalar.copy(out=first_copy[:], in_=warm[:, 0:2])
         idle = psum.tile([P, BANK], F32, name="acc")
         for i in range(WARM_UP):
             nc.tensor.matmul(out=idle[:], lhsT=warm[:, 0:P], rhs=warm[:], start=True, stop=True)
@@ -157,7 +159,6 @@ def tile_improvedattention_pa_kernel(
         head_codes(2)
         head_planes(2)
         head_codes(3)
-        load_bias(0)
         for j in range(1, 1 + W_BUFS):
             load_chunk(j)
 
@@ -189,13 +190,27 @@ def tile_improvedattention_pa_kernel(
             for g, i in order:
                 one_pass(grp[:, i, :], j, g, 2 * a + i // 2, BANK * (i % 2), BANK)
 
+        waiting = []
+
+        def store_waiting():
+            for o, third, first, a in waiting:
+                for mi in range(2):
+                    m = 2 * a + mi
+                    nc.scalar.dma_start(
+                        out=outs[third][P * m : P * (m + 1), first : first + CHUNK],
+                        in_=o[:, 2 * mi : 2 * mi + 2, :].rearrange("p i c -> p (i c)"),
+                    )
+            waiting.clear()
+
         def group_out(grp, j, a):
             third, first = chunks[j]
             o = opool.tile([P, GROUP, BANK], F32, name="o")
             for i in range(GROUP):
-                nc.vector.tensor_tensor(
-                    out=o[:, i, :], in0=grp[:, i, :], in1=bias[j][:, BANK * (i % 2) : BANK * (i % 2 + 1)], op=ADD
-                )
+                nc.scalar.copy(out=o[:, i, :], in_=grp[:, i, :])
+            store_waiting()
+            for mi in range(2):
+                row = o[:, 2 * mi : 2 * mi + 2, :].rearrange("p i c -> p (i c)")
+                nc.vector.tensor_tensor(out=row, in0=row, in1=bias[j][:], op=ADD)
             if third < 2:
                 ov = o[:].rearrange("p i (h d) -> p (i h) d", d=256)
                 t = tpool.tile([P, 2 * GROUP, 128], F32, name="t")
@@ -203,12 +218,7 @@ def tile_improvedattention_pa_kernel(
                 nc.vector.tensor_tensor(out=t[:, :, 64:128], in0=ov[:, :, 0:64], in1=sin8[:, :, 64:128], op=MULT)
                 nc.vector.tensor_tensor(out=ov[:, :, 0:128], in0=ov[:, :, 0:128], in1=cos8, op=MULT)
                 nc.vector.tensor_tensor(out=ov[:, :, 0:128], in0=ov[:, :, 0:128], in1=t[:], op=ADD)
-            for mi in range(2):
-                m = 2 * a + mi
-                nc.scalar.dma_start(
-                    out=outs[third][P * m : P * (m + 1), first : first + CHUNK],
-                    in_=o[:, 2 * mi : 2 * mi + 2, :].rearrange("p i c -> p (i c)"),
-                )
+            waiting.append((o, third, first, a))
 
         grp_a = psum.tile([P, GROUP, BANK], F32, name="acc")
         grp_b = psum.tile([P, GROUP, BANK], F32, name="acc")
@@ -231,7 +241,10 @@ def tile_improvedattention_pa_kernel(
                 group_out(grp, j, a)
             if j + W_BUFS < len(chunks):
                 load_chunk(j + W_BUFS)
+            elif j + W_BUFS == len(chunks):
+                load_bias(last)
 
+        store_waiting()
         third, first = chunks[last]
         tail = [
             [(2, 0, BANK), (2, BANK, BANK)],

@@ -24,7 +24,7 @@ W_BUFS = 5
 CODE_RUNS = ((0, 1), (1, 2), (2, 4), (4, 8))
 PLANE_RUNS = ((0, 1), (1, 4), (4, 8))
 QUADRANT_ORDER = (0, 2, 1, 3)
-WARM_UP = 8
+WARM_UP = 12
 GROUP = 4
 
 

@@ -105,7 +105,12 @@ def tile_improvedattention_pa_kernel(
             b = (j - 1) % W_BUFS
             c0 = w_col(j)
             load_scales(w_planes[b], W_qkv_scales, 0, PASSES, c0, c0 + CHUNK)
-            load_codes(w_codes[b][:], W_qkv_words, 0, PASSES, 2 * c0, 2 * (c0 + CHUNK))
+            if j == 1:
+                for g0 in (0, PASSES // 2):
+                    g1 = g0 + PASSES // 2
+                    load_codes(w_codes[b][:, g0:g1, :], W_qkv_words, g0, g1, 2 * c0, 2 * (c0 + CHUNK))
+            else:
+                load_codes(w_codes[b][:], W_qkv_words, 0, PASSES, 2 * c0, 2 * (c0 + CHUNK))
             load_bias(j - 1)
 
         zero(warm)
@@ -237,7 +242,7 @@ def tile_improvedattention_pa_kernel(
                 if j == last and a == TOKEN_TILES // 2 - 1:
                     continue
                 grp = psum.tile([P, GROUP, BANK], F32, name="acc")
-                group_passes(grp, j, a, 0, PASSES, False)
+                group_passes(grp, j, a, 0, PASSES, j == 1 and a == 0)
                 group_out(grp, j, a)
             if j + W_BUFS < len(chunks):
                 load_chunk(j + W_BUFS)

from contextlib import ExitStack

import concourse.mybir as mybir

FLOPS = 2 * 512 * 4096 * 12288

F32 = mybir.dt.float32
BF16 = mybir.dt.bfloat16
U8 = mybir.dt.uint8
I32 = mybir.dt.int32
FP4X4 = mybir.dt.float4_e2m1fn_x4
ADD = mybir.AluOpType.add
MULT = mybir.AluOpType.mult

P = 128
PASSES = 8
TOKEN_TILES = 4
BANK = 512
CHUNK = 1024
BANKS_PER_CHUNK = CHUNK // BANK
THIRD = 4096
CHUNKS_PER_THIRD = THIRD // CHUNK
W_BUFS = 5
CODE_RUNS = ((0, 1), (1, 2), (2, 4), (4, 8))
PLANE_RUNS = ((0, 1), (1, 4), (4, 8))
QUADRANT_ORDER = (0, 2, 1, 3)
WARM_UP = 12
GROUP = 4


def tile_improvedattention_pa_kernel(
    tc, x_words, x_scales, W_qkv_words, W_qkv_scales, b_qkv, sin_tab, cos_tab, out_0, out_1, out_2
):
    nc = tc.nc
    outs = [o.rearrange("b s h d -> (b s) (h d)") for o in (out_0, out_1, out_2)]
    chunks = [(third, CHUNK * i) for i in range(CHUNKS_PER_THIRD) for third in range(3)]

    with ExitStack() as ctx:
        keep = ctx.enter_context(tc.tile_pool(name="keep", bufs=1))
        opool = ctx.enter_context(tc.tile_pool(name="opool", bufs=3))
        tpool = ctx.enter_context(tc.tile_pool(name="tpool", bufs=2))
        psum = ctx.enter_context(tc.psum_pool(name="psum", bufs=2))
        ctx.enter_context(tc.manual_schedule())

        def load_codes(dst, words, g0, g1, b0, b1):
            nc.sync.dma_start(
                out=dst.bitcast(I32),
                in_=words[g0:g1, :, b0:b1].rearrange("g p n -> p g n").bitcast(I32),
            )

        def load_scales(dst, scales, g0, g1, c0, c1, quadrants=QUADRANT_ORDER):
            for q in quadrants:
                nc.sync.dma_start(
                    out=dst[32 * q : 32 * q + 4, :, :].bitcast(I32),
                    in_=scales[g0:g1, 4 * q : 4 * q + 4, c0:c1].rearrange("g r n -> r g n").bitcast(I32),
                )

        def zero(plane):
            nc.vector.memset(plane[:].bitcast(I32), 0)

        def w_col(j):
            third, c0 = chunks[j]
            return THIRD * third + c0

        x_codes = []
        w0_codes = []
        w0_planes = []
        for r, (g0, g1) in enumerate(CODE_RUNS):
            xc = keep.tile([P, g1 - g0, 2 * 512], U8, name="xc%d" % r, align_bytes=256)
            x_codes.append(xc)
            wc0 = keep.tile([P, g1 - g0, 2 * CHUNK], U8, name="w0c%d" % r, align_bytes=256)
            w0_codes.append(wc0)
        for r, (g0, g1) in enumerate(PLANE_RUNS):
            ws0 = keep.tile([P, g1 - g0, CHUNK], U8, name="w0s%d" % r, align_bytes=256)
            w0_planes.append(ws0)
        x_planes = keep.tile([P, PASSES, 512], U8, name="xs", align_bytes=256)
        w_codes = []
        w_planes = []
        for b in range(W_BUFS):
            wcb = keep.tile([P, PASSES, 2 * CHUNK], U8, name="wc%d" % b, align_bytes=256)
            w_codes.append(wcb)
            wsb = keep.tile([P, PASSES, CHUNK], U8, name="ws%d" % b, align_bytes=256)
            w_planes.append(wsb)
        bias = []
        for j in range(len(chunks)):
            bj = keep.tile([P, CHUNK], BF16, name="bias%d" % j)
            bias.append(bj)
        cos_bf = keep.tile([P, 2, 128], BF16, name="cos_bf")
        sin_bf = keep.tile([P, 2, 128], BF16, name="sin_bf")
        cos_rep = keep.tile([P, 2, 4, 128], F32, name="cos_rep")
        sin_rep = keep.tile([P, 2, 4, 128], F32, name="sin_rep")
        warm = keep.tile([P, BANK], BF16, name="warm")

        def run_of(runs, g):
            for r, (g0, g1) in enumerate(runs):
                if g0 <= g < g1:
                    return r, g - g0
            raise ValueError("no such pass")

        def load_bias(j):
            c0 = w_col(j)
            nc.sync.dma_start(out=bias[j][:], in_=b_qkv[c0 : c0 + CHUNK].partition_broadcast(P))

        def load_chunk(j):
            b = (j - 1) % W_BUFS
            c0 = w_col(j)
            load_scales(w_planes[b], W_qkv_scales, 0, PASSES, c0, c0 + CHUNK)
            if j == 1:
                for g0 in (0, PASSES // 2):
                    g1 = g0 + PASSES // 2
                    load_codes(w_codes[b][:, g0:g1, :], W_qkv_words, g0, g1, 2 * c0, 2 * (c0 + CHUNK))
            else:
                load_codes(w_codes[b][:], W_qkv_words, 0, PASSES, 2 * c0, 2 * (c0 + CHUNK))
            load_bias(j - 1)

        zero(warm)
        zero(x_planes)
        zero(w0_planes[1])
        zero(w0_planes[2])
        for b in range(W_BUFS):
            zero(w_planes[b])

        first_copy = keep.tile([P, 2], BF16, name="first_copy")
        nc.scalar.copy(out=first_copy[:], in_=warm[:, 0:2])
        idle = psum.tile([P, BANK], F32, name="acc")
        for i in range(WARM_UP):
            nc.tensor.matmul(out=idle[:], lhsT=warm[:, 0:P], rhs=warm[:], start=True, stop=True)

        nc.gpsimd.dma_start(out=cos_bf[:], in_=cos_tab.rearrange("(t p) j -> p t j", p=P))
        nc.gpsimd.dma_start(out=sin_bf[:], in_=sin_tab.rearrange("(t p) j -> p t j", p=P))
        for h in range(4):
            nc.gpsimd.tensor_copy(out=cos_rep[:, :, h, :], in_=cos_bf[:])
            nc.gpsimd.tensor_scalar(
                out=sin_rep[:, :, h, 0:64], in0=sin_bf[:, :, 0:64], scalar1=-1.0, scalar2=0.0, op0=MULT, op1=ADD
            )
            nc.gpsimd.tensor_copy(out=sin_rep[:, :, h, 64:128], in_=sin_bf[:, :, 64:128])
        cos8 = cos_rep[:].rearrange("p t k j -> p (t k) j")
        sin8 = sin_rep[:].rearrange("p t k j -> p (t k) j")

        c00 = w_col(0)
        def head_codes(r):
            g0, g1 = CODE_RUNS[r]
            load_codes(x_codes[r][:], x_words, g0, g1, 0, 1024)
            load_codes(w0_codes[r][:], W_qkv_words, g0, g1, 2 * c00, 2 * (c00 + CHUNK))

        def head_planes(r, quadrants=QUADRANT_ORDER):
            g0, g1 = PLANE_RUNS[r]
            load_scales(w0_planes[r], W_qkv_scales, g0, g1, c00, c00 + CHUNK, quadrants)

        def first_plane(quadrants):
            rows = W_qkv_scales.rearrange("g r n -> (g r) n")
            for q in quadrants:
                nc.sync.dma_start(
                    out=w0_planes[0][32 * q : 32 * q + 32, 0, :].bitcast(I32),
                    in_=rows[4 * q : 4 * q + 32, c00 : c00 + CHUNK].bitcast(I32),
                )

        first_plane(QUADRANT_ORDER[0:2])
        head_codes(0)
        first_plane(QUADRANT_ORDER[2:4])
        load_scales(x_planes, x_scales, 0, PASSES, 0, 512)
        head_codes(1)
        head_planes(1)
        head_codes(2)
        head_planes(2)
        head_codes(3)
        for j in range(1, 1 + W_BUFS):
            load_chunk(j)

        def one_pass(acc, j, g, m, c0, width):
            r, gi = run_of(CODE_RUNS, g)
            if j == 0:
                rp, gp = run_of(PLANE_RUNS, g)
                codes = w0_codes[r][:, gi, 2 * c0 : 2 * (c0 + width)]
                plane = w0_planes[rp][:, gp, c0 : c0 + width]
            else:
                b = (j - 1) % W_BUFS
                codes = w_codes[b][:, g, 2 * c0 : 2 * (c0 + width)]
                plane = w_planes[b][:, g, c0 : c0 + width]
            nc.tensor.matmul_mx(
                out=acc,
                lhsT=x_codes[r][:, gi, 2 * P * m : 2 * P * (m + 1)].bitcast(FP4X4),
                lhsT_scale=x_planes[:, g, P * m : P * (m + 1)],
                rhs=codes.bitcast(FP4X4),
                rhs_scale=plane,
                start=(g == 0),
                stop=(g == PASSES - 1),
            )

        def group_passes(grp, j, a, g0, g1, pass_outer):
            if pass_outer:
                order = [(g, i) for g in range(g0, g1) for i in range(GROUP)]
            else:
                order = [(g, i) for i in range(GROUP) for g in range(g0, g1)]
            for g, i in order:
                one_pass(grp[:, i, :], j, g, 2 * a + i // 2, BANK * (i % 2), BANK)

        waiting = []

        def store_waiting():
            for o, third, first, a in waiting:
                for mi in range(2):
                    m = 2 * a + mi
                    nc.scalar.dma_start(
                        out=outs[third][P * m : P * (m + 1), first : first + CHUNK],
                        in_=o[:, 2 * mi : 2 * mi + 2, :].rearrange("p i c -> p (i c)"),
                    )
            waiting.clear()

        def group_out(grp, j, a):
            third, first = chunks[j]
            o = opool.tile([P, GROUP, BANK], F32, name="o")
            for i in range(GROUP):
                nc.scalar.copy(out=o[:, i, :], in_=grp[:, i, :])
            store_waiting()
            for mi in range(2):
                row = o[:, 2 * mi : 2 * mi + 2, :].rearrange("p i c -> p (i c)")
                nc.vector.tensor_tensor(out=row, in0=row, in1=bias[j][:], op=ADD)
            if third < 2:
                ov = o[:].rearrange("p i (h d) -> p (i h) d", d=256)
                t = tpool.tile([P, 2 * GROUP, 128], F32, name="t")
                nc.vector.tensor_tensor(out=t[:, :, 0:64], in0=ov[:, :, 64:128], in1=sin8[:, :, 0:64], op=MULT)
                nc.vector.tensor_tensor(out=t[:, :, 64:128], in0=ov[:, :, 0:64], in1=sin8[:, :, 64:128], op=MULT)
                nc.vector.tensor_tensor(out=ov[:, :, 0:128], in0=ov[:, :, 0:128], in1=cos8, op=MULT)
                nc.vector.tensor_tensor(out=ov[:, :, 0:128], in0=ov[:, :, 0:128], in1=t[:], op=ADD)
            waiting.append((o, third, first, a))

        grp_a = psum.tile([P, GROUP, BANK], F32, name="acc")
        grp_b = psum.tile([P, GROUP, BANK], F32, name="acc")
        half = PASSES // 2
        for g in range(half):
            group_passes(grp_a, 0, 0, g, g + 1, True)
            group_passes(grp_b, 0, 1, g, g + 1, True)
        group_passes(grp_a, 0, 0, half, PASSES, True)
        group_out(grp_a, 0, 0)
        group_passes(grp_b, 0, 1, half, PASSES, True)
        group_out(grp_b, 0, 1)

        last = len(chunks) - 1
        for j in range(1, len(chunks)):
            for a in range(TOKEN_TILES // 2):
                if j == last and a == TOKEN_TILES // 2 - 1:
                    continue
                grp = psum.tile([P, GROUP, BANK], F32, name="acc")
                group_passes(grp, j, a, 0, PASSES, j == 1 and a == 0)
                group_out(grp, j, a)
            if j + W_BUFS < len(chunks):
                load_chunk(j + W_BUFS)
            elif j + W_BUFS == len(chunks):
                load_bias(last)

        store_waiting()
        third, first = chunks[last]
        tail = [
            [(2, 0, BANK), (2, BANK, BANK)],
            [(3, 0, BANK)],
            [(3, BANK, BANK // 2)],
            [(3, BANK + BANK // 2, BANK // 2)],
        ]
        for pieces in tail:
            acc = psum.tile([P, len(pieces), BANK], F32, name="acc")
            for i, (m, c0, width) in enumerate(pieces):
                for g in range(PASSES):
                    one_pass(acc[:, i, 0:width], last, g, m, c0, width)
            o = opool.tile([P, len(pieces), BANK], F32, name="o")
            for i, (m, c0, width) in enumerate(pieces):
                nc.vector.tensor_tensor(
                    out=o[:, i, 0:width], in0=acc[:, i, 0:width], in1=bias[last][:, c0 : c0 + width], op=ADD
                )
                nc.scalar.dma_start(
                    out=outs[third][P * m : P * (m + 1), first + c0 : first + c0 + width], in_=o[:, i, 0:width]
                )
